import numpy as np
import ml_dtypes


def mxq(x, axis, fmt="e4m3"):
    dtype, down = {"e4m3": (ml_dtypes.float8_e4m3fn, 7), "e5m2": (ml_dtypes.float8_e5m2, 14)}[fmt]
    v = np.moveaxis(np.asarray(x, np.float32).astype(ml_dtypes.bfloat16).astype(np.float64), axis, -1)
    blocks = v.reshape(v.shape[:-1] + (-1, 32))
    amax = np.abs(blocks).max(-1, keepdims=True)
    byte = np.maximum(np.where(amax > 0, np.frexp(amax)[1] - 1 + 127, 0) - down, 1)
    scale = np.exp2(byte - 127.0)
    codes = (blocks / scale).astype(np.float32).astype(dtype).astype(np.float64)
    return np.moveaxis((codes * scale).reshape(v.shape), -1, axis)


WIDE = False


def mx_kscale(k):
    if not WIDE:
        return np.ones(k)
    levels = np.array([10, -10, 5, -5, 0])
    a = np.random.permutation(np.resize(levels, k // 512 * 4)).reshape(k // 512, 4)
    idx = np.arange(k)
    return np.exp2(a[idx // 512, idx % 128 // 32])


BF16 = ml_dtypes.bfloat16


def bf(x):
    return np.asarray(x, np.float32).astype(BF16)


def f64(x):
    return np.asarray(x).astype(np.float64)


B, P, WS, D, H = 4, 32, 8, 512, 8
HD = D // H
WN = P // WS
N = WS * WS
SHIFT = WS // 2
LN_EPS = 1e-5


def layer_norm(x, g, b):
    mu = x.mean(-1, keepdims=True)
    var = x.var(-1, keepdims=True)
    return (x - mu) / np.sqrt(var + LN_EPS) * g + b


def window_partition(img):
    x = img.reshape(B, WN, WS, WN, WS, D).transpose(0, 1, 3, 2, 4, 5)
    return x.reshape(B * WN * WN, N, D)


def heads(t):
    return t.reshape(B * WN * WN, N, H, HD).transpose(0, 2, 1, 3)


def setup_inputs():
    s = mx_kscale(D)
    x_mid = np.random.standard_normal((B, P * P, D)) * 1.4 + np.random.standard_normal((B, P * P, 1)) * 0.5
    return {"x_mid": bf(x_mid),
            "g3": bf((1.0 + 0.1 * np.random.standard_normal(D)) * s),
            "b3": bf(0.1 * np.random.standard_normal(D) * s),
            "Wqkv2": bf(np.random.standard_normal((D, 3 * D)) / np.sqrt(D) / s[:, None]),
            "bqkv2": bf(0.1 * np.random.standard_normal(3 * D))}


def reference(x_mid, g3, b3, Wqkv2, bqkv2):
    h = layer_norm(f64(x_mid), f64(g3), f64(b3))
    img = np.roll(h.reshape(B, P, P, D), (SHIFT, SHIFT), axis=(1, 2))
    w = window_partition(img)
    qkv = (mxq(w, 2, "e4m3") @ mxq(f64(Wqkv2), 0, "e4m3")) + f64(bqkv2)
    q, k, v = np.split(qkv, 3, axis=-1)
    return heads(q), heads(k), heads(v)

@@ -1,0 +1,241 @@
+from contextlib import ExitStack
+
+import concourse.mybir as mybir
+from concourse.masks import make_identity
+
+F32 = mybir.dt.float32
+BF16 = mybir.dt.bfloat16
+U8 = mybir.dt.uint8
+U32 = mybir.dt.uint32
+FP8X4 = mybir.dt.float8_e4m3fn_x4
+ACT = mybir.ActivationFunctionType
+ALU = mybir.AluOpType
+
+P = 128
+PACK = 4
+D = 512
+IMAGES = 4
+SIDE = 32
+WS = 8
+SHIFT = 4
+HEADS = 8
+HD = 64
+WINDOWS = 16
+HALF = 4
+TG = 2
+GROUPS = WS // TG
+GROUP = TG * P
+LN_EPS = 1e-5
+
+FLOPS = 2 * IMAGES * SIDE * SIDE * D * 3 * D
+
+
+def tile_successiveswintransfomerblock_pa_t_kernel(
+    tc, x_mid, g3, b3, Wqkv2, bqkv2, out_0, out_1, out_2
+):
+    nc = tc.nc
+    with ExitStack() as ctx:
+        const = ctx.enter_context(tc.tile_pool(name="const", bufs=1))
+        x_pool = ctx.enter_context(tc.tile_pool(name="x", bufs=2 * IMAGES))
+        stat_pool = ctx.enter_context(tc.tile_pool(name="stat", bufs=6))
+        junk_pool = ctx.enter_context(tc.tile_pool(name="junk", bufs=2))
+        xn_pool = ctx.enter_context(tc.tile_pool(name="xn", bufs=4))
+        h_pool = ctx.enter_context(tc.tile_pool(name="h", bufs=3))
+        q_pool = ctx.enter_context(tc.tile_pool(name="q", bufs=2 * GROUPS))
+        o_pool = ctx.enter_context(tc.tile_pool(name="o", bufs=6))
+        psum_xt = ctx.enter_context(tc.psum_pool(name="psum_xt", bufs=2))
+        psum_acc = ctx.enter_context(tc.psum_pool(name="psum_acc", bufs=4))
+
+        def load_half(b, s):
+            x_half = x_pool.tile([P, HALF, D], BF16)
+            octets = x_mid[b].rearrange("(p jj) d -> p jj d", jj=WS)
+            nc.sync.dma_start(out=x_half[:], in_=octets[:, s * HALF : (s + 1) * HALF, :])
+            return x_half
+
+        x_halves = {}
+        x_halves[(0, 0)] = load_half(0, 0)
+        x_halves[(0, 1)] = load_half(0, 1)
+
+        gb_rows = const.tile([P, P], BF16)
+        nc.vector.memset(gb_rows[:], 0.0)
+        nc.sync.dma_start(out=gb_rows[0:PACK, :], in_=g3.rearrange("(c p) -> c p", p=P))
+        nc.sync.dma_start(out=gb_rows[PACK : 2 * PACK, :], in_=b3.rearrange("(c p) -> c p", p=P))
+
+        w_raw = const.tile([P, PACK, 3 * D], BF16)
+        nc.sync.dma_start(out=w_raw[:], in_=Wqkv2.rearrange("(c p) n -> p c n", p=P))
+
+        bias_bc = const.tile([P, 3 * D], BF16)
+        nc.sync.dma_start(out=bias_bc[:], in_=bqkv2.partition_broadcast(P))
+
+        for b in range(1, IMAGES):
+            for s in range(2):
+                x_halves[(b, s)] = load_half(b, s)
+
+        eps_col = const.tile([P, 1], F32)
+        nc.vector.memset(eps_col[:], LN_EPS)
+        warm = const.tile([P, 1], F32)
+        nc.scalar.activation(out=warm[:], in_=eps_col[:], func=ACT.Sqrt)
+
+        ident = const.tile([P, P], F32)
+        make_identity(nc, ident[:])
+
+        rolled = const.tile([P, P], F32)
+        edge = PACK * SHIFT
+        nc.vector.tensor_copy(out=rolled[:, edge:P], in_=ident[:, 0 : P - edge])
+        nc.vector.tensor_copy(out=rolled[:, 0:edge], in_=ident[:, P - edge : P])
+        rolled_v = rolled[:].rearrange("t (wr i o) -> t wr o i", wr=4, i=WS)
+        perm0 = const.tile([P, P], F32)
+        perm1 = const.tile([P, P], F32)
+        perm0_v = perm0[:].rearrange("t (wr wc i) -> t wr wc i", wr=4, wc=4)
+        perm1_v = perm1[:].rearrange("t (wr wc i) -> t wr wc i", wr=4, wc=4)
+        nc.vector.tensor_copy(out=perm0_v, in_=rolled_v)
+        nc.vector.tensor_copy(out=perm1_v[:, :, 1:4, :], in_=rolled_v[:, :, 0:3, :])
+        nc.vector.tensor_copy(out=perm1_v[:, :, 0:1, :], in_=rolled_v[:, :, 3:4, :])
+        perm = (perm0, perm1)
+
+        gb_rows_f32 = const.tile([P, P], F32)
+        nc.vector.tensor_copy(out=gb_rows_f32[:], in_=gb_rows[:])
+        gb_ps = psum_xt.tile([P, 2, GROUP], F32, name="xt0")
+        nc.tensor.transpose(gb_ps[:, 0, 0:P], gb_rows_f32[:], ident[:])
+        gb_col = const.tile([P, 2 * PACK], F32)
+        nc.vector.tensor_copy(out=gb_col[:], in_=gb_ps[:, 0, 0 : 2 * PACK])
+
+        w_grouped = const.tile([P, 3 * D, PACK], BF16, align_bytes=64)
+        w_codes = const.tile([P, 3 * D], U32, align_bytes=64)
+        w_scales = const.tile([P, 3 * D], U8, align_bytes=64)
+
+        def prepare_weight(w):
+            cols = slice(w * D, (w + 1) * D)
+            nc.scalar.copy(
+                out=w_grouped[:, cols, :], in_=w_raw[:, :, cols].rearrange("p c n -> p n c")
+            )
+            nc.vector.quantize_mx(
+                out=w_codes[:, cols].bitcast(FP8X4),
+                scales=w_scales[:, cols],
+                in_=w_grouped[:, cols, :].rearrange("p n c -> p (n c)"),
+            )
+
+        def statistics_on_vector(x_grp):
+            parts = stat_pool.tile([P, TG, 6], F32)
+            mean_var = stat_pool.tile([P, TG, 2], F32)
+            for t in range(TG):
+                nc.vector.bn_stats(out=parts[:, t, :], in_=x_grp[:, t, :])
+            for t in range(TG):
+                nc.vector.bn_aggr(out=mean_var[:, t, :], in_=parts[:, t, :])
+            negmean = stat_pool.tile([P, TG], F32)
+            nc.vector.tensor_scalar_mul(out=negmean[:], in0=mean_var[:, :, 0], scalar1=-1.0)
+            return negmean, mean_var[:, :, 1], 1.0
+
+        def statistics_on_scalar(x_grp):
+            negmean = stat_pool.tile([P, TG], F32)
+            sumsq = stat_pool.tile([P, TG], F32)
+            junk_a = junk_pool.tile([P, TG, D], BF16)
+            junk_b = junk_pool.tile([P, TG, D], BF16)
+            for t in range(TG):
+                nc.scalar.activation(
+                    out=junk_a[:, t, :], in_=x_grp[:, t, :], func=ACT.Copy,
+                    scale=-1.0 / D, accum_out=negmean[:, t : t + 1],
+                )
+            for t in range(TG):
+                nc.scalar.activation(
+                    out=junk_b[:, t, :], in_=x_grp[:, t, :], func=ACT.Square,
+                    bias=negmean[:, t : t + 1], scale=1.0, accum_out=sumsq[:, t : t + 1],
+                )
+            return negmean, sumsq[:], 1.0 / D
+
+        def normalise_and_quantise(b, g):
+            s = g * TG // HALF
+            first = g * TG - s * HALF
+            x_grp = x_halves[(b, s)][:, first : first + TG, :]
+            if b == 0:
+                negmean, spread, spread_scale = statistics_on_vector(x_grp)
+                regrouper = nc.vector
+            else:
+                negmean, spread, spread_scale = statistics_on_scalar(x_grp)
+                regrouper = nc.gpsimd
+            std = stat_pool.tile([P, TG], F32)
+            nc.scalar.activation(
+                out=std[:], in_=spread, func=ACT.Sqrt, scale=spread_scale, bias=eps_col[:, 0:1]
+            )
+            rstd = stat_pool.tile([P, TG], F32)
+            nc.vector.reciprocal(out=rstd[:], in_=std[:])
+
+            xn = xn_pool.tile([P, TG, D], F32)
+            for t in range(TG):
+                nc.gpsimd.tensor_scalar(
+                    out=xn[:, t, :], in0=x_grp[:, t, :],
+                    scalar1=negmean[:, t : t + 1], scalar2=rstd[:, t : t + 1],
+                    op0=ALU.add, op1=ALU.mult,
+                )
+
+            xt = [psum_xt.tile([P, 2, GROUP], F32, name="xt%d" % pair) for pair in range(2)]
+            for t in range(TG):
+                for c in range(PACK):
+                    nc.tensor.transpose(
+                        xt[c // 2][:, c % 2, t * P : (t + 1) * P],
+                        xn[:, t, c * P : (c + 1) * P],
+                        perm[s][:],
+                    )
+
+            h_planes = h_pool.tile([P, PACK, GROUP], BF16)
+            for c in range(PACK):
+                nc.scalar.activation(
+                    out=h_planes[:, c, :], in_=xt[c // 2][:, c % 2, :], func=ACT.Identity,
+                    scale=gb_col[:, c : c + 1], bias=gb_col[:, PACK + c : PACK + c + 1],
+                )
+            h_grouped = h_pool.tile([P, GROUP, PACK], BF16, align_bytes=64)
+            regrouper.tensor_scalar(
+                out=h_grouped[:], in0=h_planes[:].rearrange("p c m -> p m c"),
+                scalar1=1.0, scalar2=0.0, op0=ALU.mult, op1=ALU.add,
+            )
+            h_codes = q_pool.tile([P, GROUP], U32, align_bytes=64)
+            h_scales = q_pool.tile([P, GROUP], U8, align_bytes=64)
+            nc.vector.quantize_mx(
+                out=h_codes[:].bitcast(FP8X4),
+                scales=h_scales[:],
+                in_=h_grouped[:].rearrange("p m c -> p (m c)"),
+            )
+            return h_codes, h_scales
+
+        def project_and_store(b, quantised):
+            for w, out_w in enumerate((out_0, out_1, out_2)):
+                cols = slice(w * D, (w + 1) * D)
+                o_tile = o_pool.tile([P, HEADS, WS, HD], F32)
+                for g in range(GROUPS):
+                    h_codes, h_scales = quantised[g]
+                    for t in range(TG):
+                        j = (g * TG + t + SHIFT) % WS
+                        tokens = slice(t * P, (t + 1) * P)
+                        acc = psum_acc.tile([P, D], F32)
+                        nc.tensor.matmul_mx(
+                            out=acc[:],
+                            lhsT=h_codes[:, tokens].bitcast(FP8X4),
+                            lhsT_scale=h_scales[:, tokens],
+                            rhs=w_codes[:, cols].bitcast(FP8X4),
+                            rhs_scale=w_scales[:, cols],
+                            start=True,
+                            stop=True,
+                        )
+                        nc.vector.tensor_tensor(
+                            out=o_tile[:, :, j, :],
+                            in0=acc[:].rearrange("p (h f) -> p h f", h=HEADS),
+                            in1=bias_bc[:, cols].rearrange("p (h f) -> p h f", h=HEADS),
+                            op=ALU.add,
+                        )
+                for head in range(HEADS):
+                    rows = out_w[b * WINDOWS : (b + 1) * WINDOWS, head]
+                    nc.sync.dma_start(
+                        out=rows.rearrange("w (i j) f -> w i (j f)", i=WS),
+                        in_=o_tile[:, head].rearrange("p j f -> p (j f)"),
+                    )
+
+        prepare_weight(0)
+        quantised = [normalise_and_quantise(0, g) for g in range(GROUPS)]
+        prepare_weight(1)
+        prepare_weight(2)
+        for b in range(IMAGES):
+            following = []
+            if b + 1 < IMAGES:
+                following = [normalise_and_quantise(b + 1, g) for g in range(GROUPS)]
+            project_and_store(b, quantised)
+            quantised = following

@@ -106,7 +106,7 @@ def tile_successiveswintransfomerblock_pa_t_kernel(
 
         def prepare_weight(w):
             cols = slice(w * D, (w + 1) * D)
-            nc.scalar.copy(
+            nc.vector.tensor_copy(
                 out=w_grouped[:, cols, :], in_=w_raw[:, :, cols].rearrange("p c n -> p n c")
             )
             nc.vector.quantize_mx(
@@ -143,22 +143,29 @@ def tile_successiveswintransfomerblock_pa_t_kernel(
                 )
             return negmean, sumsq[:], 1.0 / D
 
-        def normalise_and_quantise(b, g):
+        def tokens_of_group(b, g):
             s = g * TG // HALF
             first = g * TG - s * HALF
-            x_grp = x_halves[(b, s)][:, first : first + TG, :]
+            return x_halves[(b, s)][:, first : first + TG, :]
+
+        def statistics(b, g):
+            x_grp = tokens_of_group(b, g)
             if b == 0:
                 negmean, spread, spread_scale = statistics_on_vector(x_grp)
-                regrouper = nc.vector
             else:
                 negmean, spread, spread_scale = statistics_on_scalar(x_grp)
-                regrouper = nc.gpsimd
             std = stat_pool.tile([P, TG], F32)
             nc.scalar.activation(
                 out=std[:], in_=spread, func=ACT.Sqrt, scale=spread_scale, bias=eps_col[:, 0:1]
             )
             rstd = stat_pool.tile([P, TG], F32)
             nc.vector.reciprocal(out=rstd[:], in_=std[:])
+            return negmean, rstd
+
+        def normalise_and_quantise(b, g, negmean, rstd):
+            s = g * TG // HALF
+            x_grp = tokens_of_group(b, g)
+            regrouper = nc.vector if b == 0 else nc.gpsimd
 
             xn = xn_pool.tile([P, TG, D], F32)
             for t in range(TG):
@@ -199,6 +206,8 @@ def tile_successiveswintransfomerblock_pa_t_kernel(
 
         def project_and_store(b, quantised):
             for w, out_w in enumerate((out_0, out_1, out_2)):
+                if b == 0 and w > 0:
+                    prepare_weight(w)
                 cols = slice(w * D, (w + 1) * D)
                 o_tile = o_pool.tile([P, HEADS, WS, HD], F32)
                 for g in range(GROUPS):
@@ -229,13 +238,15 @@ def tile_successiveswintransfomerblock_pa_t_kernel(
                         in_=o_tile[:, head].rearrange("p j f -> p (j f)"),
                     )
 
+        def layer_norm_of_image(b):
+            return [normalise_and_quantise(b, g, *statistics(b, g)) for g in range(GROUPS)]
+
+        first_stats = [statistics(0, g) for g in range(GROUPS)]
         prepare_weight(0)
-        quantised = [normalise_and_quantise(0, g) for g in range(GROUPS)]
-        prepare_weight(1)
-        prepare_weight(2)
+        quantised = [normalise_and_quantise(0, g, *first_stats[g]) for g in range(GROUPS)]
         for b in range(IMAGES):
             following = []
             if b + 1 < IMAGES:
-                following = [normalise_and_quantise(b + 1, g) for g in range(GROUPS)]
+                following = layer_norm_of_image(b + 1)
             project_and_store(b, quantised)
             quantised = following

@@ -106,8 +106,9 @@ def tile_successiveswintransfomerblock_pa_t_kernel(
 
         def prepare_weight(w):
             cols = slice(w * D, (w + 1) * D)
-            nc.vector.tensor_copy(
-                out=w_grouped[:, cols, :], in_=w_raw[:, :, cols].rearrange("p c n -> p n c")
+            nc.gpsimd.tensor_scalar(
+                out=w_grouped[:, cols, :], in0=w_raw[:, :, cols].rearrange("p c n -> p n c"),
+                scalar1=1.0, scalar2=0.0, op0=ALU.mult, op1=ALU.add,
             )
             nc.vector.quantize_mx(
                 out=w_codes[:, cols].bitcast(FP8X4),
@@ -143,13 +144,10 @@ def tile_successiveswintransfomerblock_pa_t_kernel(
                 )
             return negmean, sumsq[:], 1.0 / D
 
-        def tokens_of_group(b, g):
+        def normalise_and_quantise(b, g):
             s = g * TG // HALF
             first = g * TG - s * HALF
-            return x_halves[(b, s)][:, first : first + TG, :]
-
-        def statistics(b, g):
-            x_grp = tokens_of_group(b, g)
+            x_grp = x_halves[(b, s)][:, first : first + TG, :]
             if b == 0:
                 negmean, spread, spread_scale = statistics_on_vector(x_grp)
             else:
@@ -160,19 +158,14 @@ def tile_successiveswintransfomerblock_pa_t_kernel(
             )
             rstd = stat_pool.tile([P, TG], F32)
             nc.vector.reciprocal(out=rstd[:], in_=std[:])
-            return negmean, rstd
-
-        def normalise_and_quantise(b, g, negmean, rstd):
-            s = g * TG // HALF
-            x_grp = tokens_of_group(b, g)
-            regrouper = nc.vector if b == 0 else nc.gpsimd
+            shift = stat_pool.tile([P, TG], F32)
+            nc.vector.tensor_mul(out=shift[:], in0=negmean[:], in1=rstd[:])
 
             xn = xn_pool.tile([P, TG, D], F32)
             for t in range(TG):
-                nc.gpsimd.tensor_scalar(
-                    out=xn[:, t, :], in0=x_grp[:, t, :],
-                    scalar1=negmean[:, t : t + 1], scalar2=rstd[:, t : t + 1],
-                    op0=ALU.add, op1=ALU.mult,
+                nc.scalar.activation(
+                    out=xn[:, t, :], in_=x_grp[:, t, :], func=ACT.Identity,
+                    scale=rstd[:, t : t + 1], bias=shift[:, t : t + 1],
                 )
 
             xt = [psum_xt.tile([P, 2, GROUP], F32, name="xt%d" % pair) for pair in range(2)]
@@ -191,7 +184,7 @@ def tile_successiveswintransfomerblock_pa_t_kernel(
                     scale=gb_col[:, c : c + 1], bias=gb_col[:, PACK + c : PACK + c + 1],
                 )
             h_grouped = h_pool.tile([P, GROUP, PACK], BF16, align_bytes=64)
-            regrouper.tensor_scalar(
+            nc.gpsimd.tensor_scalar(
                 out=h_grouped[:], in0=h_planes[:].rearrange("p c m -> p m c"),
                 scalar1=1.0, scalar2=0.0, op0=ALU.mult, op1=ALU.add,
             )
@@ -206,8 +199,6 @@ def tile_successiveswintransfomerblock_pa_t_kernel(
 
         def project_and_store(b, quantised):
             for w, out_w in enumerate((out_0, out_1, out_2)):
-                if b == 0 and w > 0:
-                    prepare_weight(w)
                 cols = slice(w * D, (w + 1) * D)
                 o_tile = o_pool.tile([P, HEADS, WS, HD], F32)
                 for g in range(GROUPS):
@@ -238,15 +229,13 @@ def tile_successiveswintransfomerblock_pa_t_kernel(
                         in_=o_tile[:, head].rearrange("p j f -> p (j f)"),
                     )
 
-        def layer_norm_of_image(b):
-            return [normalise_and_quantise(b, g, *statistics(b, g)) for g in range(GROUPS)]
-
-        first_stats = [statistics(0, g) for g in range(GROUPS)]
         prepare_weight(0)
-        quantised = [normalise_and_quantise(0, g, *first_stats[g]) for g in range(GROUPS)]
+        quantised = [normalise_and_quantise(0, g) for g in range(GROUPS)]
+        prepare_weight(1)
+        prepare_weight(2)
         for b in range(IMAGES):
             following = []
             if b + 1 < IMAGES:
-                following = layer_norm_of_image(b + 1)
+                following = [normalise_and_quantise(b + 1, g) for g in range(GROUPS)]
             project_and_store(b, quantised)
             quantised = following

@@ -20,10 +20,12 @@ WS = 8
 SHIFT = 4
 HEADS = 8
 HD = 64
-WINDOWS = 16
-HALF = 4
+QUAD = 4
+QUADS = SIDE // QUAD
+UNIT_ROWS = P // QUADS
+UNIT_WINDOWS = 8
+UNITS = 2 * IMAGES
 TG = 2
-GROUPS = WS // TG
 GROUP = TG * P
 LN_EPS = 1e-5
 
@@ -36,25 +38,31 @@ def tile_successiveswintransfomerblock_pa_t_kernel(
     nc = tc.nc
     with ExitStack() as ctx:
         const = ctx.enter_context(tc.tile_pool(name="const", bufs=1))
-        x_pool = ctx.enter_context(tc.tile_pool(name="x", bufs=2 * IMAGES))
+        x_pool = ctx.enter_context(tc.tile_pool(name="x", bufs=UNITS))
         stat_pool = ctx.enter_context(tc.tile_pool(name="stat", bufs=6))
         junk_pool = ctx.enter_context(tc.tile_pool(name="junk", bufs=2))
         xn_pool = ctx.enter_context(tc.tile_pool(name="xn", bufs=4))
         h_pool = ctx.enter_context(tc.tile_pool(name="h", bufs=3))
-        q_pool = ctx.enter_context(tc.tile_pool(name="q", bufs=2 * GROUPS))
-        o_pool = ctx.enter_context(tc.tile_pool(name="o", bufs=6))
+        q_pool = ctx.enter_context(tc.tile_pool(name="q", bufs=6))
+        o_pool = ctx.enter_context(tc.tile_pool(name="o", bufs=10))
         psum_xt = ctx.enter_context(tc.psum_pool(name="psum_xt", bufs=2))
         psum_acc = ctx.enter_context(tc.psum_pool(name="psum_acc", bufs=4))
 
-        def load_half(b, s):
-            x_half = x_pool.tile([P, HALF, D], BF16)
-            octets = x_mid[b].rearrange("(p jj) d -> p jj d", jj=WS)
-            nc.sync.dma_start(out=x_half[:], in_=octets[:, s * HALF : (s + 1) * HALF, :])
-            return x_half
+        def load_unit(u):
+            x_unit = x_pool.tile([P, QUAD, D], BF16)
+            quads = x_mid[u // 2].rearrange("(t jl) d -> t jl d", jl=QUAD)
+            first_row = (u % 2) * UNIT_ROWS - SHIFT
+            if first_row < 0:
+                wrapped = -first_row * QUADS
+                nc.sync.dma_start(out=x_unit[0:wrapped], in_=quads[SIDE * QUADS - wrapped :])
+                nc.sync.dma_start(out=x_unit[wrapped:P], in_=quads[0 : P - wrapped])
+            else:
+                nc.sync.dma_start(
+                    out=x_unit[:], in_=quads[first_row * QUADS : first_row * QUADS + P]
+                )
+            return x_unit
 
-        x_halves = {}
-        x_halves[(0, 0)] = load_half(0, 0)
-        x_halves[(0, 1)] = load_half(0, 1)
+        x_units = [load_unit(0), load_unit(1)]
 
         gb_rows = const.tile([P, P], BF16)
         nc.vector.memset(gb_rows[:], 0.0)
@@ -67,9 +75,8 @@ def tile_successiveswintransfomerblock_pa_t_kernel(
         bias_bc = const.tile([P, 3 * D], BF16)
         nc.sync.dma_start(out=bias_bc[:], in_=bqkv2.partition_broadcast(P))
 
-        for b in range(1, IMAGES):
-            for s in range(2):
-                x_halves[(b, s)] = load_half(b, s)
+        for u in range(2, UNITS):
+            x_units.append(load_unit(u))
 
         eps_col = const.tile([P, 1], F32)
         nc.vector.memset(eps_col[:], LN_EPS)
@@ -79,19 +86,16 @@ def tile_successiveswintransfomerblock_pa_t_kernel(
         ident = const.tile([P, P], F32)
         make_identity(nc, ident[:])
 
-        rolled = const.tile([P, P], F32)
-        edge = PACK * SHIFT
-        nc.vector.tensor_copy(out=rolled[:, edge:P], in_=ident[:, 0 : P - edge])
-        nc.vector.tensor_copy(out=rolled[:, 0:edge], in_=ident[:, P - edge : P])
-        rolled_v = rolled[:].rearrange("t (wr i o) -> t wr o i", wr=4, i=WS)
-        perm0 = const.tile([P, P], F32)
-        perm1 = const.tile([P, P], F32)
-        perm0_v = perm0[:].rearrange("t (wr wc i) -> t wr wc i", wr=4, wc=4)
-        perm1_v = perm1[:].rearrange("t (wr wc i) -> t wr wc i", wr=4, wc=4)
-        nc.vector.tensor_copy(out=perm0_v, in_=rolled_v)
-        nc.vector.tensor_copy(out=perm1_v[:, :, 1:4, :], in_=rolled_v[:, :, 0:3, :])
-        nc.vector.tensor_copy(out=perm1_v[:, :, 0:1, :], in_=rolled_v[:, :, 3:4, :])
-        perm = (perm0, perm1)
+        shifted = const.tile([P, P], F32)
+        ident_v = ident[:].rearrange("t (r q) -> t r q", q=QUADS)
+        shifted_v = shifted[:].rearrange("t (r q) -> t r q", q=QUADS)
+        nc.vector.tensor_copy(out=shifted_v[:, :, 1:QUADS], in_=ident_v[:, :, 0 : QUADS - 1])
+        nc.vector.tensor_copy(out=shifted_v[:, :, 0:1], in_=ident_v[:, :, QUADS - 1 : QUADS])
+        perm = const.tile([P, P], F32)
+        perm_v = perm[:].rearrange("t (i jh wr wc) -> t jh i wr wc", i=WS, jh=2, wr=2)
+        from_v = shifted[:].rearrange("t (wr i wc jh) -> t jh i wr wc", wr=2, i=WS, wc=4)
+        for jh in range(2):
+            nc.vector.tensor_copy(out=perm_v[:, jh], in_=from_v[:, jh])
 
         gb_rows_f32 = const.tile([P, P], F32)
         nc.vector.tensor_copy(out=gb_rows_f32[:], in_=gb_rows[:])
@@ -106,9 +110,8 @@ def tile_successiveswintransfomerblock_pa_t_kernel(
 
         def prepare_weight(w):
             cols = slice(w * D, (w + 1) * D)
-            nc.gpsimd.tensor_scalar(
-                out=w_grouped[:, cols, :], in0=w_raw[:, :, cols].rearrange("p c n -> p n c"),
-                scalar1=1.0, scalar2=0.0, op0=ALU.mult, op1=ALU.add,
+            nc.scalar.copy(
+                out=w_grouped[:, cols, :], in_=w_raw[:, :, cols].rearrange("p c n -> p n c")
             )
             nc.vector.quantize_mx(
                 out=w_codes[:, cols].bitcast(FP8X4),
@@ -144,28 +147,27 @@ def tile_successiveswintransfomerblock_pa_t_kernel(
                 )
             return negmean, sumsq[:], 1.0 / D
 
-        def normalise_and_quantise(b, g):
-            s = g * TG // HALF
-            first = g * TG - s * HALF
-            x_grp = x_halves[(b, s)][:, first : first + TG, :]
-            if b == 0:
+        def normalise_and_quantise(u, g):
+            x_grp = x_units[u][:, g * TG : (g + 1) * TG, :]
+            if u < 2:
                 negmean, spread, spread_scale = statistics_on_vector(x_grp)
+                regrouper = nc.vector
             else:
                 negmean, spread, spread_scale = statistics_on_scalar(x_grp)
+                regrouper = nc.gpsimd
             std = stat_pool.tile([P, TG], F32)
             nc.scalar.activation(
                 out=std[:], in_=spread, func=ACT.Sqrt, scale=spread_scale, bias=eps_col[:, 0:1]
             )
             rstd = stat_pool.tile([P, TG], F32)
             nc.vector.reciprocal(out=rstd[:], in_=std[:])
-            shift = stat_pool.tile([P, TG], F32)
-            nc.vector.tensor_mul(out=shift[:], in0=negmean[:], in1=rstd[:])
 
             xn = xn_pool.tile([P, TG, D], F32)
             for t in range(TG):
-                nc.scalar.activation(
-                    out=xn[:, t, :], in_=x_grp[:, t, :], func=ACT.Identity,
-                    scale=rstd[:, t : t + 1], bias=shift[:, t : t + 1],
+                nc.gpsimd.tensor_scalar(
+                    out=xn[:, t, :], in0=x_grp[:, t, :],
+                    scalar1=negmean[:, t : t + 1], scalar2=rstd[:, t : t + 1],
+                    op0=ALU.add, op1=ALU.mult,
                 )
 
             xt = [psum_xt.tile([P, 2, GROUP], F32, name="xt%d" % pair) for pair in range(2)]
@@ -174,7 +176,7 @@ def tile_successiveswintransfomerblock_pa_t_kernel(
                     nc.tensor.transpose(
                         xt[c // 2][:, c % 2, t * P : (t + 1) * P],
                         xn[:, t, c * P : (c + 1) * P],
-                        perm[s][:],
+                        perm[:],
                     )
 
             h_planes = h_pool.tile([P, PACK, GROUP], BF16)
@@ -184,7 +186,7 @@ def tile_successiveswintransfomerblock_pa_t_kernel(
                     scale=gb_col[:, c : c + 1], bias=gb_col[:, PACK + c : PACK + c + 1],
                 )
             h_grouped = h_pool.tile([P, GROUP, PACK], BF16, align_bytes=64)
-            nc.gpsimd.tensor_scalar(
+            regrouper.tensor_scalar(
                 out=h_grouped[:], in0=h_planes[:].rearrange("p c m -> p m c"),
                 scalar1=1.0, scalar2=0.0, op0=ALU.mult, op1=ALU.add,
             )
@@ -197,45 +199,45 @@ def tile_successiveswintransfomerblock_pa_t_kernel(
             )
             return h_codes, h_scales
 
-        def project_and_store(b, quantised):
+        def project_and_store(u, quantised):
+            windows = slice(u * UNIT_WINDOWS, (u + 1) * UNIT_WINDOWS)
             for w, out_w in enumerate((out_0, out_1, out_2)):
                 cols = slice(w * D, (w + 1) * D)
-                o_tile = o_pool.tile([P, HEADS, WS, HD], F32)
-                for g in range(GROUPS):
-                    h_codes, h_scales = quantised[g]
-                    for t in range(TG):
-                        j = (g * TG + t + SHIFT) % WS
-                        tokens = slice(t * P, (t + 1) * P)
-                        acc = psum_acc.tile([P, D], F32)
-                        nc.tensor.matmul_mx(
-                            out=acc[:],
-                            lhsT=h_codes[:, tokens].bitcast(FP8X4),
-                            lhsT_scale=h_scales[:, tokens],
-                            rhs=w_codes[:, cols].bitcast(FP8X4),
-                            rhs_scale=w_scales[:, cols],
-                            start=True,
-                            stop=True,
-                        )
-                        nc.vector.tensor_tensor(
-                            out=o_tile[:, :, j, :],
-                            in0=acc[:].rearrange("p (h f) -> p h f", h=HEADS),
-                            in1=bias_bc[:, cols].rearrange("p (h f) -> p h f", h=HEADS),
-                            op=ALU.add,
-                        )
-                for head in range(HEADS):
-                    rows = out_w[b * WINDOWS : (b + 1) * WINDOWS, head]
-                    nc.sync.dma_start(
-                        out=rows.rearrange("w (i j) f -> w i (j f)", i=WS),
-                        in_=o_tile[:, head].rearrange("p j f -> p (j f)"),
+                o_tile = o_pool.tile([P, HEADS, QUAD, HD], F32)
+                for jl in range(QUAD):
+                    h_codes, h_scales = quantised[jl // TG]
+                    tokens = slice((jl % TG) * P, (jl % TG + 1) * P)
+                    acc = psum_acc.tile([P, D], F32)
+                    nc.tensor.matmul_mx(
+                        out=acc[:],
+                        lhsT=h_codes[:, tokens].bitcast(FP8X4),
+                        lhsT_scale=h_scales[:, tokens],
+                        rhs=w_codes[:, cols].bitcast(FP8X4),
+                        rhs_scale=w_scales[:, cols],
+                        start=True,
+                        stop=True,
                     )
+                    nc.vector.tensor_tensor(
+                        out=o_tile[:, :, jl, :],
+                        in0=acc[:].rearrange("p (h f) -> p h f", h=HEADS),
+                        in1=bias_bc[:, cols].rearrange("p (h f) -> p h f", h=HEADS),
+                        op=ALU.add,
+                    )
+                nc.sync.dma_start(
+                    out=out_w[windows].rearrange("w h (x jl) f -> x (w h) (jl f)", jl=QUAD),
+                    in_=o_tile[:].rearrange("p h jl f -> p h (jl f)"),
+                )
+
+        def layer_norm_of_unit(u):
+            return [normalise_and_quantise(u, g) for g in range(QUAD // TG)]
 
         prepare_weight(0)
-        quantised = [normalise_and_quantise(0, g) for g in range(GROUPS)]
+        quantised = layer_norm_of_unit(0)
         prepare_weight(1)
         prepare_weight(2)
-        for b in range(IMAGES):
+        for u in range(UNITS):
             following = []
-            if b + 1 < IMAGES:
-                following = [normalise_and_quantise(b + 1, g) for g in range(GROUPS)]
-            project_and_store(b, quantised)
+            if u + 1 < UNITS:
+                following = layer_norm_of_unit(u + 1)
+            project_and_store(u, quantised)
             quantised = following

@@ -27,6 +27,7 @@ UNIT_WINDOWS = 8
 UNITS = 2 * IMAGES
 TG = 2
 GROUP = TG * P
+LEAD = 2
 LN_EPS = 1e-5
 
 FLOPS = 2 * IMAGES * SIDE * SIDE * D * 3 * D
@@ -43,7 +44,7 @@ def tile_successiveswintransfomerblock_pa_t_kernel(
         junk_pool = ctx.enter_context(tc.tile_pool(name="junk", bufs=2))
         xn_pool = ctx.enter_context(tc.tile_pool(name="xn", bufs=4))
         h_pool = ctx.enter_context(tc.tile_pool(name="h", bufs=3))
-        q_pool = ctx.enter_context(tc.tile_pool(name="q", bufs=6))
+        q_pool = ctx.enter_context(tc.tile_pool(name="q", bufs=8))
         o_pool = ctx.enter_context(tc.tile_pool(name="o", bufs=10))
         psum_xt = ctx.enter_context(tc.psum_pool(name="psum_xt", bufs=2))
         psum_acc = ctx.enter_context(tc.psum_pool(name="psum_acc", bufs=4))
@@ -232,12 +233,10 @@ def tile_successiveswintransfomerblock_pa_t_kernel(
             return [normalise_and_quantise(u, g) for g in range(QUAD // TG)]
 
         prepare_weight(0)
-        quantised = layer_norm_of_unit(0)
+        quantised = [layer_norm_of_unit(u) for u in range(LEAD)]
         prepare_weight(1)
         prepare_weight(2)
         for u in range(UNITS):
-            following = []
-            if u + 1 < UNITS:
-                following = layer_norm_of_unit(u + 1)
-            project_and_store(u, quantised)
-            quantised = following
+            if u + LEAD < UNITS:
+                quantised.append(layer_norm_of_unit(u + LEAD))
+            project_and_store(u, quantised[u])

@@ -52,7 +52,7 @@ def tile_successiveswintransfomerblock_pa_t_kernel(
         def load_unit(u):
             x_unit = x_pool.tile([P, QUAD, D], BF16)
             quads = x_mid[u // 2].rearrange("(t jl) d -> t jl d", jl=QUAD)
-            first_row = (u % 2) * UNIT_ROWS - SHIFT
+            first_row = (1 - u % 2) * UNIT_ROWS - SHIFT
             if first_row < 0:
                 wrapped = -first_row * QUADS
                 nc.sync.dma_start(out=x_unit[0:wrapped], in_=quads[SIDE * QUADS - wrapped :])
@@ -111,9 +111,11 @@ def tile_successiveswintransfomerblock_pa_t_kernel(
 
         def prepare_weight(w):
             cols = slice(w * D, (w + 1) * D)
-            nc.scalar.copy(
-                out=w_grouped[:, cols, :], in_=w_raw[:, :, cols].rearrange("p c n -> p n c")
-            )
+            by_column = w_raw[:, :, cols].rearrange("p c n -> p n c")
+            if w == 0:
+                nc.vector.tensor_copy(out=w_grouped[:, cols, :], in_=by_column)
+            else:
+                nc.scalar.copy(out=w_grouped[:, cols, :], in_=by_column)
             nc.vector.quantize_mx(
                 out=w_codes[:, cols].bitcast(FP8X4),
                 scales=w_scales[:, cols],
@@ -201,7 +203,8 @@ def tile_successiveswintransfomerblock_pa_t_kernel(
             return h_codes, h_scales
 
         def project_and_store(u, quantised):
-            windows = slice(u * UNIT_WINDOWS, (u + 1) * UNIT_WINDOWS)
+            first_window = (u // 2 * 2 + 1 - u % 2) * UNIT_WINDOWS
+            windows = slice(first_window, first_window + UNIT_WINDOWS)
             for w, out_w in enumerate((out_0, out_1, out_2)):
                 cols = slice(w * D, (w + 1) * D)
                 o_tile = o_pool.tile([P, HEADS, QUAD, HD], F32)

@@ -52,7 +52,7 @@ def tile_successiveswintransfomerblock_pa_t_kernel(
         def load_unit(u):
             x_unit = x_pool.tile([P, QUAD, D], BF16)
             quads = x_mid[u // 2].rearrange("(t jl) d -> t jl d", jl=QUAD)
-            first_row = (1 - u % 2) * UNIT_ROWS - SHIFT
+            first_row = (u % 2) * UNIT_ROWS - SHIFT
             if first_row < 0:
                 wrapped = -first_row * QUADS
                 nc.sync.dma_start(out=x_unit[0:wrapped], in_=quads[SIDE * QUADS - wrapped :])
@@ -152,7 +152,7 @@ def tile_successiveswintransfomerblock_pa_t_kernel(
 
         def normalise_and_quantise(u, g):
             x_grp = x_units[u][:, g * TG : (g + 1) * TG, :]
-            if u < 2:
+            if u < 1:
                 negmean, spread, spread_scale = statistics_on_vector(x_grp)
                 regrouper = nc.vector
             else:
@@ -203,8 +203,7 @@ def tile_successiveswintransfomerblock_pa_t_kernel(
             return h_codes, h_scales
 
         def project_and_store(u, quantised):
-            first_window = (u // 2 * 2 + 1 - u % 2) * UNIT_WINDOWS
-            windows = slice(first_window, first_window + UNIT_WINDOWS)
+            windows = slice(u * UNIT_WINDOWS, (u + 1) * UNIT_WINDOWS)
             for w, out_w in enumerate((out_0, out_1, out_2)):
                 cols = slice(w * D, (w + 1) * D)
                 o_tile = o_pool.tile([P, HEADS, QUAD, HD], F32)

from contextlib import ExitStack

import concourse.mybir as mybir
from concourse.masks import make_identity

F32 = mybir.dt.float32
BF16 = mybir.dt.bfloat16
U8 = mybir.dt.uint8
U32 = mybir.dt.uint32
FP8X4 = mybir.dt.float8_e4m3fn_x4
ACT = mybir.ActivationFunctionType
ALU = mybir.AluOpType

P = 128
PACK = 4
D = 512
IMAGES = 4
SIDE = 32
WS = 8
SHIFT = 4
HEADS = 8
HD = 64
QUAD = 4
QUADS = SIDE // QUAD
UNIT_ROWS = P // QUADS
UNIT_WINDOWS = 8
UNITS = 2 * IMAGES
TG = 2
GROUP = TG * P
LEAD = 2
LN_EPS = 1e-5

FLOPS = 2 * IMAGES * SIDE * SIDE * D * 3 * D


def tile_successiveswintransfomerblock_pa_t_kernel(
    tc, x_mid, g3, b3, Wqkv2, bqkv2, out_0, out_1, out_2
):
    nc = tc.nc
    with ExitStack() as ctx:
        const = ctx.enter_context(tc.tile_pool(name="const", bufs=1))
        x_pool = ctx.enter_context(tc.tile_pool(name="x", bufs=UNITS))
        stat_pool = ctx.enter_context(tc.tile_pool(name="stat", bufs=6))
        junk_pool = ctx.enter_context(tc.tile_pool(name="junk", bufs=2))
        xn_pool = ctx.enter_context(tc.tile_pool(name="xn", bufs=4))
        h_pool = ctx.enter_context(tc.tile_pool(name="h", bufs=3))
        q_pool = ctx.enter_context(tc.tile_pool(name="q", bufs=8))
        o_pool = ctx.enter_context(tc.tile_pool(name="o", bufs=10))
        psum_xt = ctx.enter_context(tc.psum_pool(name="psum_xt", bufs=2))
        psum_acc = ctx.enter_context(tc.psum_pool(name="psum_acc", bufs=4))

        def load_unit(u):
            x_unit = x_pool.tile([P, QUAD, D], BF16)
            quads = x_mid[u // 2].rearrange("(t jl) d -> t jl d", jl=QUAD)
            first_row = (u % 2) * UNIT_ROWS - SHIFT
            if first_row < 0:
                wrapped = -first_row * QUADS
                nc.sync.dma_start(out=x_unit[0:wrapped], in_=quads[SIDE * QUADS - wrapped :])
                nc.sync.dma_start(out=x_unit[wrapped:P], in_=quads[0 : P - wrapped])
            else:
                nc.sync.dma_start(
                    out=x_unit[:], in_=quads[first_row * QUADS : first_row * QUADS + P]
                )
            return x_unit

        x_units = [load_unit(0), load_unit(1)]

        gb_rows = const.tile([P, P], BF16)
        nc.vector.memset(gb_rows[:], 0.0)
        nc.sync.dma_start(out=gb_rows[0:PACK, :], in_=g3.rearrange("(c p) -> c p", p=P))
        nc.sync.dma_start(out=gb_rows[PACK : 2 * PACK, :], in_=b3.rearrange("(c p) -> c p", p=P))

        w_raw = const.tile([P, PACK, 3 * D], BF16)
        nc.sync.dma_start(out=w_raw[:], in_=Wqkv2.rearrange("(c p) n -> p c n", p=P))

        bias_bc = const.tile([P, 3 * D], BF16)
        nc.sync.dma_start(out=bias_bc[:], in_=bqkv2.partition_broadcast(P))

        for u in range(2, UNITS):
            x_units.append(load_unit(u))

        eps_col = const.tile([P, 1], F32)
        nc.vector.memset(eps_col[:], LN_EPS)
        warm = const.tile([P, 1], F32)
        nc.scalar.activation(out=warm[:], in_=eps_col[:], func=ACT.Sqrt)

        ident = const.tile([P, P], F32)
        make_identity(nc, ident[:])

        shifted = const.tile([P, P], F32)
        ident_v = ident[:].rearrange("t (r q) -> t r q", q=QUADS)
        shifted_v = shifted[:].rearrange("t (r q) -> t r q", q=QUADS)
        nc.vector.tensor_copy(out=shifted_v[:, :, 1:QUADS], in_=ident_v[:, :, 0 : QUADS - 1])
        nc.vector.tensor_copy(out=shifted_v[:, :, 0:1], in_=ident_v[:, :, QUADS - 1 : QUADS])
        perm = const.tile([P, P], F32)
        perm_v = perm[:].rearrange("t (i jh wr wc) -> t jh i wr wc", i=WS, jh=2, wr=2)
        from_v = shifted[:].rearrange("t (wr i wc jh) -> t jh i wr wc", wr=2, i=WS, wc=4)
        for jh in range(2):
            nc.vector.tensor_copy(out=perm_v[:, jh], in_=from_v[:, jh])

        gb_rows_f32 = const.tile([P, P], F32)
        nc.vector.tensor_copy(out=gb_rows_f32[:], in_=gb_rows[:])
        gb_ps = psum_xt.tile([P, 2, GROUP], F32, name="xt0")
        nc.tensor.transpose(gb_ps[:, 0, 0:P], gb_rows_f32[:], ident[:])
        gb_col = const.tile([P, 2 * PACK], F32)
        nc.vector.tensor_copy(out=gb_col[:], in_=gb_ps[:, 0, 0 : 2 * PACK])

        w_grouped = const.tile([P, 3 * D, PACK], BF16, align_bytes=64)
        w_codes = const.tile([P, 3 * D], U32, align_bytes=64)
        w_scales = const.tile([P, 3 * D], U8, align_bytes=64)

        def prepare_weight(w):
            cols = slice(w * D, (w + 1) * D)
            by_column = w_raw[:, :, cols].rearrange("p c n -> p n c")
            if w == 0:
                nc.vector.tensor_copy(out=w_grouped[:, cols, :], in_=by_column)
            else:
                nc.scalar.copy(out=w_grouped[:, cols, :], in_=by_column)
            nc.vector.quantize_mx(
                out=w_codes[:, cols].bitcast(FP8X4),
                scales=w_scales[:, cols],
                in_=w_grouped[:, cols, :].rearrange("p n c -> p (n c)"),
            )

        def statistics_on_vector(x_grp):
            parts = stat_pool.tile([P, TG, 6], F32)
            mean_var = stat_pool.tile([P, TG, 2], F32)
            for t in range(TG):
                nc.vector.bn_stats(out=parts[:, t, :], in_=x_grp[:, t, :])
            for t in range(TG):
                nc.vector.bn_aggr(out=mean_var[:, t, :], in_=parts[:, t, :])
            negmean = stat_pool.tile([P, TG], F32)
            nc.vector.tensor_scalar_mul(out=negmean[:], in0=mean_var[:, :, 0], scalar1=-1.0)
            return negmean, mean_var[:, :, 1], 1.0

        def statistics_on_scalar(x_grp):
            negmean = stat_pool.tile([P, TG], F32)
            sumsq = stat_pool.tile([P, TG], F32)
            junk_a = junk_pool.tile([P, TG, D], BF16)
            junk_b = junk_pool.tile([P, TG, D], BF16)
            for t in range(TG):
                nc.scalar.activation(
                    out=junk_a[:, t, :], in_=x_grp[:, t, :], func=ACT.Copy,
                    scale=-1.0 / D, accum_out=negmean[:, t : t + 1],
                )
            for t in range(TG):
                nc.scalar.activation(
                    out=junk_b[:, t, :], in_=x_grp[:, t, :], func=ACT.Square,
                    bias=negmean[:, t : t + 1], scale=1.0, accum_out=sumsq[:, t : t + 1],
                )
            return negmean, sumsq[:], 1.0 / D

        def normalise_and_quantise(u, g):
            x_grp = x_units[u][:, g * TG : (g + 1) * TG, :]
            if u < 1:
                negmean, spread, spread_scale = statistics_on_vector(x_grp)
                regrouper = nc.vector
            else:
                negmean, spread, spread_scale = statistics_on_scalar(x_grp)
                regrouper = nc.gpsimd
            std = stat_pool.tile([P, TG], F32)
            nc.scalar.activation(
                out=std[:], in_=spread, func=ACT.Sqrt, scale=spread_scale, bias=eps_col[:, 0:1]
            )
            rstd = stat_pool.tile([P, TG], F32)
            nc.vector.reciprocal(out=rstd[:], in_=std[:])

            xn = xn_pool.tile([P, TG, D], F32)
            for t in range(TG):
                nc.gpsimd.tensor_scalar(
                    out=xn[:, t, :], in0=x_grp[:, t, :],
                    scalar1=negmean[:, t : t + 1], scalar2=rstd[:, t : t + 1],
                    op0=ALU.add, op1=ALU.mult,
                )

            xt = [psum_xt.tile([P, 2, GROUP], F32, name="xt%d" % pair) for pair in range(2)]
            for t in range(TG):
                for c in range(PACK):
                    nc.tensor.transpose(
                        xt[c // 2][:, c % 2, t * P : (t + 1) * P],
                        xn[:, t, c * P : (c + 1) * P],
                        perm[:],
                    )

            h_planes = h_pool.tile([P, PACK, GROUP], BF16)
            for c in range(PACK):
                nc.scalar.activation(
                    out=h_planes[:, c, :], in_=xt[c // 2][:, c % 2, :], func=ACT.Identity,
                    scale=gb_col[:, c : c + 1], bias=gb_col[:, PACK + c : PACK + c + 1],
                )
            h_grouped = h_pool.tile([P, GROUP, PACK], BF16, align_bytes=64)
            regrouper.tensor_scalar(
                out=h_grouped[:], in0=h_planes[:].rearrange("p c m -> p m c"),
                scalar1=1.0, scalar2=0.0, op0=ALU.mult, op1=ALU.add,
            )
            h_codes = q_pool.tile([P, GROUP], U32, align_bytes=64)
            h_scales = q_pool.tile([P, GROUP], U8, align_bytes=64)
            nc.vector.quantize_mx(
                out=h_codes[:].bitcast(FP8X4),
                scales=h_scales[:],
                in_=h_grouped[:].rearrange("p m c -> p (m c)"),
            )
            return h_codes, h_scales

        def project_and_store(u, quantised):
            windows = slice(u * UNIT_WINDOWS, (u + 1) * UNIT_WINDOWS)
            for w, out_w in enumerate((out_0, out_1, out_2)):
                cols = slice(w * D, (w + 1) * D)
                o_tile = o_pool.tile([P, HEADS, QUAD, HD], F32)
                for jl in range(QUAD):
                    h_codes, h_scales = quantised[jl // TG]
                    tokens = slice((jl % TG) * P, (jl % TG + 1) * P)
                    acc = psum_acc.tile([P, D], F32)
                    nc.tensor.matmul_mx(
                        out=acc[:],
                        lhsT=h_codes[:, tokens].bitcast(FP8X4),
                        lhsT_scale=h_scales[:, tokens],
                        rhs=w_codes[:, cols].bitcast(FP8X4),
                        rhs_scale=w_scales[:, cols],
                        start=True,
                        stop=True,
                    )
                    nc.vector.tensor_tensor(
                        out=o_tile[:, :, jl, :],
                        in0=acc[:].rearrange("p (h f) -> p h f", h=HEADS),
                        in1=bias_bc[:, cols].rearrange("p (h f) -> p h f", h=HEADS),
                        op=ALU.add,
                    )
                nc.sync.dma_start(
                    out=out_w[windows].rearrange("w h (x jl) f -> x (w h) (jl f)", jl=QUAD),
                    in_=o_tile[:].rearrange("p h jl f -> p h (jl f)"),
                )

        def layer_norm_of_unit(u):
            return [normalise_and_quantise(u, g) for g in range(QUAD // TG)]

        prepare_weight(0)
        quantised = [layer_norm_of_unit(u) for u in range(LEAD)]
        prepare_weight(1)
        prepare_weight(2)
        for u in range(UNITS):
            if u + LEAD < UNITS:
                quantised.append(layer_norm_of_unit(u + LEAD))
            project_and_store(u, quantised[u])
